import numpy as np
import ml_dtypes


def mxq(x, axis, fmt="e4m3"):
    dtype, down = {"e4m3": (ml_dtypes.float8_e4m3fn, 7), "e5m2": (ml_dtypes.float8_e5m2, 14)}[fmt]
    v = np.moveaxis(np.asarray(x, np.float32).astype(ml_dtypes.bfloat16).astype(np.float64), axis, -1)
    blocks = v.reshape(v.shape[:-1] + (-1, 32))
    amax = np.abs(blocks).max(-1, keepdims=True)
    byte = np.maximum(np.where(amax > 0, np.frexp(amax)[1] - 1 + 127, 0) - down, 1)
    scale = np.exp2(byte - 127.0)
    codes = (blocks / scale).astype(np.float32).astype(dtype).astype(np.float64)
    return np.moveaxis((codes * scale).reshape(v.shape), -1, axis)


WIDE = False


def mx_kscale(k):
    if not WIDE:
        return np.ones(k)
    levels = np.array([18, -18])
    if k % 512:
        return np.exp2(np.random.permutation(np.resize(levels, k // 32))).repeat(32)
    a = np.empty((k // 512, 16))
    for p in range(k // 512):
        a[p, :8] = np.random.permutation(np.resize(levels, 8))
        for g in range(8):
            far = levels[np.abs(levels - a[p, g]) >= 10]
            a[p, g + 8] = far[np.random.randint(len(far))]
    return np.exp2(a.ravel()).repeat(32)


BF16 = ml_dtypes.bfloat16


def bf(x):
    return np.asarray(x, np.float32).astype(BF16)


def f64(x):
    return np.asarray(x).astype(np.float64)


D_DIM, T_DIM, M_DIM = 1024, 1536, 1536
C_INIT = 1.0


def setup_inputs():
    s = mx_kscale(T_DIM)[None, :]
    u = mx_kscale(D_DIM)[:, None]
    Z = bf(0.2 * np.random.standard_normal((D_DIM, T_DIM)))
    x0 = bf(np.random.standard_normal((M_DIM, T_DIM)))
    U = bf(2.0 / np.sqrt(D_DIM) * np.random.standard_normal((D_DIM, D_DIM)))
    v0 = bf(0.4 / np.sqrt(M_DIM) * np.random.standard_normal((D_DIM, M_DIM)))
    l1 = bf(np.random.uniform(0.08, 0.12, 1))
    g = bf(4.0 * np.random.standard_normal((D_DIM, T_DIM)) * np.exp2(np.random.randint(-6, 1, (1, T_DIM))) / s * u)
    mat = f64(U) @ f64(Z) + f64(v0) @ f64(x0)
    return {"Z": Z,
            "X": bf(f64(x0) * s),
            "U": U,
            "V": bf(f64(v0) / u),
            "l1": l1,
            "mat": np.asarray(mat, np.float32),
            "grad_out": g}


def reference(Z, X, U, V, l1, mat, grad_out):
    thres = f64(l1) / C_INIT
    dmat = np.where(np.abs(f64(mat)) > thres, f64(grad_out), 0.0)
    dX = mxq(f64(V), 0, "e4m3").T @ mxq(dmat, 0, "e5m2")
    dV = mxq(dmat, 1, "e5m2") @ mxq(f64(X), 1, "e4m3").T
    return dX, dV

@@ -1,0 +1,312 @@
+from contextlib import ExitStack
+
+import concourse.mybir as mybir
+from concourse.masks import make_identity
+
+D, T, M = 1024, 1536, 1536
+FLOPS = 2 * 2 * D * T * M
+BYTES = 2 * (M * T + D * M + D * T) + 4 * (D * T + M * T + D * M) + 2
+
+F32 = mybir.dt.float32
+BF16 = mybir.dt.bfloat16
+U32 = mybir.dt.uint32
+U8 = mybir.dt.uint8
+E4M3 = mybir.dt.float8_e4m3fn_x4
+E5M2 = mybir.dt.float8_e5m2_x4
+ALU = mybir.AluOpType
+ABS = mybir.ActivationFunctionType.Abs
+
+P = 128
+K = 512
+N = 512
+DG = D // K
+TG = T // K
+MC = M // N
+
+
+def tile_blueboxlayer_pb_v_kernel(tc, Z, X, U, V, l1, mat, grad_out, out_0, out_1):
+    nc = tc.nc
+    with ExitStack() as ctx:
+        const = ctx.enter_context(tc.tile_pool(name="const", bufs=1))
+        raw = ctx.enter_context(tc.tile_pool(name="raw", bufs=7))
+        keep = ctx.enter_context(tc.tile_pool(name="keep", bufs=1))
+        work = ctx.enter_context(tc.tile_pool(name="work", bufs=3))
+        outs = ctx.enter_context(tc.tile_pool(name="outs", bufs=2))
+        psum = ctx.enter_context(tc.psum_pool(name="psum", bufs=8))
+        ctx.enter_context(tc.manual_schedule())
+
+        thres = const.tile([P, 1], BF16, name="thres")
+        nc.scalar.dma_start(out=thres[:], in_=l1.partition_broadcast(P))
+        ident = const.tile([P, P], F32, name="ident")
+        make_identity(nc, ident[:])
+
+        mat_v = mat.rearrange("(g p j) t -> g p j t", g=DG, j=4)
+        grad_v = grad_out.rearrange("(g p j) t -> g p j t", g=DG, j=4)
+        v_v = V.rearrange("(g p j) m -> g p j m", g=DG, j=4)
+        x_v = X.rearrange("(b i p) t -> b p i t", i=2, p=P)
+        mats, grads, xs, vs = {}, {}, {}, {}
+
+        def load_mat(g, j):
+            t = raw.tile([P, T], F32, name="mat_raw", tag="raw")
+            nc.sync.dma_start(out=t[:], in_=mat_v[g, :, j, :])
+            mats[g, j] = t
+
+        def load_grad(g, h):
+            t = raw.tile([P, 2, T], BF16, name="grad_raw", tag="raw")
+            nc.sync.dma_start(out=t[:], in_=grad_v[g, :, 2 * h : 2 * h + 2, :])
+            grads[g, h] = t
+
+        def load_g(g):
+            load_mat(g, 0)
+            load_grad(g, 0)
+            load_mat(g, 1)
+            load_mat(g, 2)
+            load_grad(g, 1)
+            load_mat(g, 3)
+
+        load_g(0)
+        for b in range(6):
+            t = raw.tile([P, 2, T], BF16, name="x_raw", tag="raw")
+            nc.sync.dma_start(out=t[:], in_=x_v[b])
+            xs[b] = t
+        load_g(1)
+        for g in range(DG):
+            t = keep.tile([P, 4, M], BF16, name="v_raw%d" % g)
+            nc.sync.dma_start(out=t[:], in_=v_v[g])
+            vs[g] = t
+
+        dmat = [keep.tile([P, 4, T], BF16, name="dmat%d" % g) for g in range(DG)]
+        dt_codes = [keep.tile([P, TG, K], U32, name="dt_codes%d" % g, align_bytes=64) for g in range(DG)]
+        dt_scales = [keep.tile([P, TG, K], U8, name="dt_scales%d" % g, align_bytes=64) for g in range(DG)]
+        x_codes = [keep.tile([P, TG, N], U32, name="x_codes%d" % c, align_bytes=64) for c in range(MC)]
+        x_scales = [keep.tile([P, TG, N], U8, name="x_scales%d" % c, align_bytes=64) for c in range(MC)]
+        d_codes = [keep.tile([P, DG, N], U32, name="d_codes%d" % s, align_bytes=64) for s in range(TG)]
+        d_scales = [keep.tile([P, DG, N], U8, name="d_scales%d" % s, align_bytes=64) for s in range(TG)]
+        v_codes = [keep.tile([P, DG, N], U32, name="v_codes%d" % c, align_bytes=64) for c in range(MC)]
+        v_scales = [keep.tile([P, DG, N], U8, name="v_scales%d" % c, align_bytes=64) for c in range(MC)]
+
+        def evac(engine, out, in_):
+            if engine == "S":
+                nc.scalar.copy(out=out, in_=in_)
+            else:
+                nc.vector.tensor_copy(out=out, in_=in_)
+
+        def absolute(g, j):
+            nc.scalar.activation(out=mats[g, j][:], in_=mats[g, j][:], func=ABS)
+
+        def mask(g, j):
+            for u in range(2):
+                nc.vector.scalar_tensor_tensor(
+                    out=dmat[g][:, j, :].rearrange("p (s u q e) -> p s u q e", s=TG, u=2, e=2)[:, :, u],
+                    in0=mats[g, j][:].rearrange("p (s q u e) -> p s q u e", s=TG, u=2, e=2)[:, :, :, u],
+                    scalar=thres[:, 0:1],
+                    in1=grads[g, j // 2][:, j % 2, :].rearrange("p (s q u e) -> p s q u e", s=TG, u=2, e=2)[:, :, :, u],
+                    op0=ALU.is_gt, op1=ALU.mult)
+
+        dt_rows, x_rows = {}, {}
+
+        def transpose_pair(word, engines, rows):
+            for s in range(TG):
+                bank = psum.tile([P, 4, P], F32, name="bank_t", tag="bank")
+                for i in range(2):
+                    for u in range(2):
+                        nc.tensor.transpose(bank[:, 2 * i + u, :], word(i, s, u), ident[:])
+                evac(engines[s], rows(s), bank[:].rearrange("q (i u) p -> q i p u", u=2))
+
+        def words_of(tile_view):
+            return tile_view.rearrange("p i t -> p (i t)").bitcast(F32)
+
+        def transpose_d(g, h, engines):
+            if h == 0:
+                for s in range(TG):
+                    dt_rows[g, s] = work.tile([P, K * 4], BF16, name="dt_rows", tag="dt_rows", align_bytes=64)
+
+            def rows(s):
+                return dt_rows[g, s][:].bitcast(F32).rearrange("q (i p u) -> q i p u", i=4, u=2)[:, 2 * h : 2 * h + 2]
+
+            words = words_of(dmat[g][:, 2 * h : 2 * h + 2, :])
+
+            def word(i, s, u):
+                first = i * (T // 2) + 256 * s + 128 * u
+                return words[:, first : first + 128]
+
+            transpose_pair(word, engines, rows)
+
+        def quantize_dt(g, s):
+            nc.vector.quantize_mx(out=dt_codes[g][:, s, :].bitcast(E5M2), scales=dt_scales[g][:, s, :], in_=dt_rows[g, s][:])
+
+        def transpose_x(b, engines):
+            c = b // 2
+            if b % 2 == 0:
+                for s in range(TG):
+                    x_rows[c, s] = work.tile([P, N * 4], BF16, name="x_rows", tag="x_rows", bufs=6, align_bytes=64)
+
+            def rows(s):
+                return x_rows[c, s][:].bitcast(F32).rearrange("q (i p u) -> q i p u", i=4, u=2)[:, 2 * (b % 2) : 2 * (b % 2) + 2]
+
+            words = words_of(xs[b][:])
+
+            def word(i, s, u):
+                first = i * (T // 2) + 256 * s + u
+                return words[:, first : first + 255 : 2]
+
+            transpose_pair(word, engines, rows)
+
+        def quantize_x(c, s):
+            nc.vector.quantize_mx(out=x_codes[c][:, s, :].bitcast(E4M3), scales=x_scales[c][:, s, :], in_=x_rows[c, s][:])
+
+        grouped = {}
+
+        def group(key, src, cols):
+            t = work.tile([P, N, 4], BF16, name="grouped", tag="grouped", bufs=2, align_bytes=64)
+            nc.vector.tensor_copy(
+                out=t[:].rearrange("p (c i) j -> p c j i", i=4),
+                in_=src[:, :, cols].rearrange("p j (c i) -> p c j i", i=4))
+            grouped[key] = t
+
+        def group_d(g, s):
+            group(("d", g, s), dmat[g], slice(s * N, s * N + N))
+
+        def quantize_d(g, s):
+            nc.vector.quantize_mx(out=d_codes[s][:, g, :].bitcast(E5M2), scales=d_scales[s][:, g, :],
+                                  in_=grouped["d", g, s][:].rearrange("p n j -> p (n j)"))
+
+        def group_v(g, c):
+            group(("v", g, c), vs[g], slice(c * N, c * N + N))
+
+        def quantize_v(g, c):
+            nc.vector.quantize_mx(out=v_codes[c][:, g, :].bitcast(E4M3), scales=v_scales[c][:, g, :],
+                                  in_=grouped["v", g, c][:].rearrange("p n j -> p (n j)"))
+
+        out_1v = out_1.rearrange("(g p j) m -> g p j m", g=DG, j=4)
+
+        def product_1(g, c, h, engines):
+            stage = outs.tile([P, 2, N], F32, name="stage1", tag="stage", bufs=8)
+            for i in range(2):
+                j = 2 * h + i
+                bank = psum.tile([P, N], F32, name="bank_1", tag="bank")
+                for s in range(TG):
+                    cols = slice(j * P, j * P + P)
+                    nc.tensor.matmul_mx(
+                        out=bank[:], lhsT=dt_codes[g][:, s, cols].bitcast(E5M2), lhsT_scale=dt_scales[g][:, s, cols],
+                        rhs=x_codes[c][:, s, :].bitcast(E4M3), rhs_scale=x_scales[c][:, s, :],
+                        start=(s == 0), stop=(s == TG - 1))
+                evac(engines[i], stage[:, i, :], bank[:])
+            nc.sync.dma_start(out=out_1v[g, :, 2 * h : 2 * h + 2, c * N : c * N + N], in_=stage[:])
+
+        out_0v = out_0.rearrange("(c b p) t -> c p b t", c=MC, p=P)
+
+        def product_0(c, s, h, engines, pieces=1):
+            stage = outs.tile([P, 2, N], F32, name="stage0", tag="stage", bufs=8)
+            toks = slice(s * N, s * N + N)
+            for i in range(2):
+                b = 2 * h + i
+                cols = slice(b * P, b * P + P)
+                bank = psum.tile([P, N], F32, name="bank_0", tag="bank")
+                for g in range(DG):
+                    nc.tensor.matmul_mx(
+                        out=bank[:], lhsT=v_codes[c][:, g, cols].bitcast(E4M3), lhsT_scale=v_scales[c][:, g, cols],
+                        rhs=d_codes[s][:, g, :].bitcast(E5M2), rhs_scale=d_scales[s][:, g, :],
+                        start=(g == 0), stop=(g == DG - 1))
+                evac(engines[i], stage[:, i, :].rearrange("p (q u e) -> p q u e", u=2, e=2),
+                     bank[:].rearrange("p (u q e) -> p q u e", u=2, e=2))
+                if pieces == 2:
+                    nc.sync.dma_start(out=out_0v[c, :, b, toks], in_=stage[:, i, :])
+            if pieces == 1:
+                nc.sync.dma_start(out=out_0v[c, :, 2 * h : 2 * h + 2, toks], in_=stage[:])
+
+        absolute(0, 0)
+        mask(0, 0)
+        absolute(0, 1)
+        absolute(0, 2)
+        mask(0, 1)
+        absolute(0, 3)
+        transpose_d(0, 0, "SSV")
+        mask(0, 2)
+        mask(0, 3)
+        transpose_x(0, "SVS")
+        transpose_x(1, "SVS")
+        group_d(0, 0)
+        transpose_d(0, 1, "SVS")
+        quantize_x(0, 0)
+        quantize_x(0, 1)
+        quantize_x(0, 2)
+        transpose_x(2, "SVS")
+        quantize_dt(0, 0)
+        quantize_dt(0, 1)
+        quantize_dt(0, 2)
+        transpose_x(3, "SSS")
+        quantize_x(1, 0)
+        transpose_x(4, "SVS")
+        quantize_x(1, 1)
+        quantize_x(1, 2)
+        transpose_x(5, "SVS")
+        absolute(1, 0)
+        quantize_x(2, 0)
+        quantize_x(2, 1)
+        quantize_x(2, 2)
+        product_1(0, 0, 0, "SS")
+        absolute(1, 1)
+        mask(1, 0)
+        product_1(0, 0, 1, "SS")
+        mask(1, 1)
+        product_1(0, 1, 0, "SV")
+        absolute(1, 2)
+        quantize_d(0, 0)
+        product_1(0, 1, 1, "SS")
+        mask(1, 2)
+        absolute(1, 3)
+        transpose_d(1, 0, "SVS")
+        product_1(0, 2, 0, "SS")
+        mask(1, 3)
+        transpose_d(1, 1, "SVS")
+        group_d(1, 0)
+        quantize_dt(1, 0)
+        quantize_dt(1, 1)
+        quantize_dt(1, 2)
+        product_1(0, 2, 1, "SS")
+        group_v(0, 0)
+        quantize_d(1, 0)
+        product_1(1, 0, 0, "SS")
+        quantize_v(0, 0)
+        group_v(1, 0)
+        product_1(1, 0, 1, "SS")
+        quantize_v(1, 0)
+        group_d(0, 1)
+        product_1(1, 1, 0, "SS")
+        group_d(1, 1)
+        quantize_d(0, 1)
+        product_0(0, 0, 0, "SS", 1)
+        product_0(0, 0, 1, "SS", 1)
+        product_1(1, 1, 1, "SS")
+        quantize_d(1, 1)
+        group_v(0, 1)
+        product_1(1, 2, 0, "SS")
+        product_0(0, 1, 0, "SS", 1)
+        group_v(1, 1)
+        quantize_v(0, 1)
+        product_0(0, 1, 1, "SS", 1)
+        product_1(1, 2, 1, "SS")
+        group_d(0, 2)
+        quantize_v(1, 1)
+        group_d(1, 2)
+        quantize_d(0, 2)
+        product_0(1, 0, 0, "SS", 1)
+        quantize_d(1, 2)
+        group_v(0, 2)
+        product_0(1, 0, 1, "SS", 1)
+        group_v(1, 2)
+        quantize_v(0, 2)
+        product_0(1, 1, 0, "SS", 1)
+        quantize_v(1, 2)
+        product_0(1, 1, 1, "SV", 1)
+        product_0(0, 2, 0, "SV", 1)
+        product_0(0, 2, 1, "SV", 1)
+        product_0(1, 2, 0, "SV", 1)
+        product_0(1, 2, 1, "SV", 1)
+        product_0(2, 0, 0, "SV", 1)
+        product_0(2, 0, 1, "SV", 1)
+        product_0(2, 1, 0, "SV", 1)
+        product_0(2, 1, 1, "SV", 1)
+        product_0(2, 2, 0, "SV", 1)
+        product_0(2, 2, 1, "SV", 2)

@@ -11,6 +11,7 @@ F32 = mybir.dt.float32
 BF16 = mybir.dt.bfloat16
 U32 = mybir.dt.uint32
 U8 = mybir.dt.uint8
+I32 = mybir.dt.int32
 E4M3 = mybir.dt.float8_e4m3fn_x4
 E5M2 = mybir.dt.float8_e5m2_x4
 ALU = mybir.AluOpType
@@ -28,10 +29,10 @@ def tile_blueboxlayer_pb_v_kernel(tc, Z, X, U, V, l1, mat, grad_out, out_0, out_
     nc = tc.nc
     with ExitStack() as ctx:
         const = ctx.enter_context(tc.tile_pool(name="const", bufs=1))
-        raw = ctx.enter_context(tc.tile_pool(name="raw", bufs=7))
+        raw = ctx.enter_context(tc.tile_pool(name="raw", bufs=5))
         keep = ctx.enter_context(tc.tile_pool(name="keep", bufs=1))
         work = ctx.enter_context(tc.tile_pool(name="work", bufs=3))
-        outs = ctx.enter_context(tc.tile_pool(name="outs", bufs=2))
+        outs = ctx.enter_context(tc.tile_pool(name="outs", bufs=7))
         psum = ctx.enter_context(tc.psum_pool(name="psum", bufs=8))
         ctx.enter_context(tc.manual_schedule())
 
@@ -43,39 +44,47 @@ def tile_blueboxlayer_pb_v_kernel(tc, Z, X, U, V, l1, mat, grad_out, out_0, out_
         mat_v = mat.rearrange("(g p j) t -> g p j t", g=DG, j=4)
         grad_v = grad_out.rearrange("(g p j) t -> g p j t", g=DG, j=4)
         v_v = V.rearrange("(g p j) m -> g p j m", g=DG, j=4)
-        x_v = X.rearrange("(b i p) t -> b p i t", i=2, p=P)
+        x_v = X.rearrange("(c p i) t -> c p i t", c=MC, i=4)
         mats, grads, xs, vs = {}, {}, {}, {}
 
-        def load_mat(g, j):
-            t = raw.tile([P, T], F32, name="mat_raw", tag="raw")
-            nc.sync.dma_start(out=t[:], in_=mat_v[g, :, j, :])
-            mats[g, j] = t
+        def raw_tile(store, key, shape, dtype):
+            if key not in store:
+                store[key] = raw.tile(shape, dtype, name="raw_tile", tag="raw", align_bytes=64)
+            return store[key]
 
-        def load_grad(g, h):
-            t = raw.tile([P, 2, T], BF16, name="grad_raw", tag="raw")
-            nc.sync.dma_start(out=t[:], in_=grad_v[g, :, 2 * h : 2 * h + 2, :])
-            grads[g, h] = t
+        def load_mat(g, j, n=1):
+            t = raw_tile(mats, (g, j // 2), [P, 2, T], F32)
+            nc.sync.dma_start(out=t[:, j % 2 : j % 2 + n, :], in_=mat_v[g, :, j : j + n, :])
 
-        def load_g(g):
-            load_mat(g, 0)
-            load_grad(g, 0)
-            load_mat(g, 1)
-            load_mat(g, 2)
-            load_grad(g, 1)
-            load_mat(g, 3)
+        def load_grad(g, h, n=1):
+            t = raw_tile(grads, g, [P, 4, T], BF16)
+            nc.sync.dma_start(out=t[:, 2 * h : 2 * h + 2 * n, :], in_=grad_v[g, :, 2 * h : 2 * h + 2 * n, :])
 
-        load_g(0)
-        for b in range(6):
-            t = raw.tile([P, 2, T], BF16, name="x_raw", tag="raw")
-            nc.sync.dma_start(out=t[:], in_=x_v[b])
-            xs[b] = t
-        load_g(1)
-        for g in range(DG):
-            t = keep.tile([P, 4, M], BF16, name="v_raw%d" % g)
+        def load_x(b, n=1):
+            t = raw_tile(xs, b // 2, [P, 4, T], BF16)
+            i = 2 * (b % 2)
+            nc.sync.dma_start(out=t[:, i : i + 2 * n, :], in_=x_v[b // 2, :, i : i + 2 * n, :])
+
+        def load_v(g):
+            t = raw_tile(vs, g, [P, 4, M], BF16)
             nc.sync.dma_start(out=t[:], in_=v_v[g])
-            vs[g] = t
 
-        dmat = [keep.tile([P, 4, T], BF16, name="dmat%d" % g) for g in range(DG)]
+        load_mat(0, 0)
+        load_grad(0, 0)
+        load_mat(0, 1)
+        load_x(0)
+        load_x(1)
+        load_mat(0, 2)
+        load_grad(0, 1)
+        load_mat(0, 3)
+        load_x(2, 2)
+        load_x(4, 2)
+        load_mat(1, 0, 2)
+        load_grad(1, 0, 2)
+        load_mat(1, 2, 2)
+        load_v(0)
+        load_v(1)
+        dmat = [keep.tile([P, 4, T], BF16, name="dmat%d" % g, align_bytes=64) for g in range(DG)]
         dt_codes = [keep.tile([P, TG, K], U32, name="dt_codes%d" % g, align_bytes=64) for g in range(DG)]
         dt_scales = [keep.tile([P, TG, K], U8, name="dt_scales%d" % g, align_bytes=64) for g in range(DG)]
         x_codes = [keep.tile([P, TG, N], U32, name="x_codes%d" % c, align_bytes=64) for c in range(MC)]
@@ -91,66 +100,61 @@ def tile_blueboxlayer_pb_v_kernel(tc, Z, X, U, V, l1, mat, grad_out, out_0, out_
             else:
                 nc.vector.tensor_copy(out=out, in_=in_)
 
-        def absolute(g, j):
-            nc.scalar.activation(out=mats[g, j][:], in_=mats[g, j][:], func=ABS)
+        def absolute(g, j, engine):
+            row = mats[g, j // 2][:, j % 2, :]
+            if engine == "S":
+                nc.scalar.activation(out=row, in_=row, func=ABS)
+            else:
+                bits = row.bitcast(I32)
+                nc.vector.tensor_scalar(out=bits, in0=bits, scalar1=0x7FFFFFFF, scalar2=None, op0=ALU.bitwise_and)
 
         def mask(g, j):
             for u in range(2):
                 nc.vector.scalar_tensor_tensor(
                     out=dmat[g][:, j, :].rearrange("p (s u q e) -> p s u q e", s=TG, u=2, e=2)[:, :, u],
-                    in0=mats[g, j][:].rearrange("p (s q u e) -> p s q u e", s=TG, u=2, e=2)[:, :, :, u],
+                    in0=mats[g, j // 2][:, j % 2, :].rearrange("p (s q u e) -> p s q u e", s=TG, u=2, e=2)[:, :, :, u],
                     scalar=thres[:, 0:1],
-                    in1=grads[g, j // 2][:, j % 2, :].rearrange("p (s q u e) -> p s q u e", s=TG, u=2, e=2)[:, :, :, u],
+                    in1=grads[g][:, j, :].rearrange("p (s q u e) -> p s q u e", s=TG, u=2, e=2)[:, :, :, u],
                     op0=ALU.is_gt, op1=ALU.mult)
 
         dt_rows, x_rows = {}, {}
 
-        def transpose_pair(word, engines, rows):
+        def words_of(rows):
+            return rows.rearrange("p i t -> p (i t)").bitcast(F32)
+
+        def transpose_d(g, h, engines):
+            words = words_of(dmat[g][:, 2 * h : 2 * h + 2, :])
             for s in range(TG):
+                if h == 0:
+                    dt_rows[g, s] = work.tile([P, K * 4], BF16, name="dt_rows", tag="dt_rows", align_bytes=64)
                 bank = psum.tile([P, 4, P], F32, name="bank_t", tag="bank")
                 for i in range(2):
                     for u in range(2):
-                        nc.tensor.transpose(bank[:, 2 * i + u, :], word(i, s, u), ident[:])
-                evac(engines[s], rows(s), bank[:].rearrange("q (i u) p -> q i p u", u=2))
+                        first = i * (T // 2) + 256 * s + 128 * u
+                        nc.tensor.transpose(bank[:, 2 * i + u, :], words[:, first : first + 128], ident[:])
+                evac(engines[s],
+                     dt_rows[g, s][:].bitcast(F32).rearrange("q (i p u) -> q i p u", i=4, u=2)[:, 2 * h : 2 * h + 2],
+                     bank[:].rearrange("q (i u) p -> q i p u", u=2))
 
-        def words_of(tile_view):
-            return tile_view.rearrange("p i t -> p (i t)").bitcast(F32)
-
-        def transpose_d(g, h, engines):
-            if h == 0:
-                for s in range(TG):
-                    dt_rows[g, s] = work.tile([P, K * 4], BF16, name="dt_rows", tag="dt_rows", align_bytes=64)
-
-            def rows(s):
-                return dt_rows[g, s][:].bitcast(F32).rearrange("q (i p u) -> q i p u", i=4, u=2)[:, 2 * h : 2 * h + 2]
-
-            words = words_of(dmat[g][:, 2 * h : 2 * h + 2, :])
-
-            def word(i, s, u):
-                first = i * (T // 2) + 256 * s + 128 * u
-                return words[:, first : first + 128]
-
-            transpose_pair(word, engines, rows)
-
-        def quantize_dt(g, s):
-            nc.vector.quantize_mx(out=dt_codes[g][:, s, :].bitcast(E5M2), scales=dt_scales[g][:, s, :], in_=dt_rows[g, s][:])
+        def quantize_dt(g, s, h):
+            half = slice(h * K // 2, (h + 1) * K // 2)
+            nc.vector.quantize_mx(out=dt_codes[g][:, s, half].bitcast(E5M2), scales=dt_scales[g][:, s, half],
+                                  in_=dt_rows[g, s][:, h * 2 * K : (h + 1) * 2 * K])
 
         def transpose_x(b, engines):
-            c = b // 2
-            if b % 2 == 0:
-                for s in range(TG):
-                    x_rows[c, s] = work.tile([P, N * 4], BF16, name="x_rows", tag="x_rows", bufs=6, align_bytes=64)
-
-            def rows(s):
-                return x_rows[c, s][:].bitcast(F32).rearrange("q (i p u) -> q i p u", i=4, u=2)[:, 2 * (b % 2) : 2 * (b % 2) + 2]
-
-            words = words_of(xs[b][:])
-
-            def word(i, s, u):
-                first = i * (T // 2) + 256 * s + u
-                return words[:, first : first + 255 : 2]
-
-            transpose_pair(word, engines, rows)
+            c, h = b // 2, b % 2
+            words = words_of(xs[c][:, 2 * h : 2 * h + 2, :])
+            for s in range(TG):
+                if h == 0:
+                    x_rows[c, s] = work.tile([P, N * 4], BF16, name="x_rows", tag="x_rows", bufs=5, align_bytes=64)
+                bank = psum.tile([P, 4, P], F32, name="bank_t", tag="bank")
+                for i in range(2):
+                    for u in range(2):
+                        first = i * (T // 2) + 256 * s + u
+                        nc.tensor.transpose(bank[:, 2 * i + u, :], words[:, first : first + 255 : 2], ident[:])
+                evac(engines[s],
+                     x_rows[c, s][:].bitcast(F32).rearrange("q (p h w) -> q p h w", h=2, w=4)[:, :, h],
+                     bank[:].rearrange("q w p -> q p w"))
 
         def quantize_x(c, s):
             nc.vector.quantize_mx(out=x_codes[c][:, s, :].bitcast(E4M3), scales=x_scales[c][:, s, :], in_=x_rows[c, s][:])
@@ -178,135 +182,176 @@ def tile_blueboxlayer_pb_v_kernel(tc, Z, X, U, V, l1, mat, grad_out, out_0, out_
             nc.vector.quantize_mx(out=v_codes[c][:, g, :].bitcast(E4M3), scales=v_scales[c][:, g, :],
                                   in_=grouped["v", g, c][:].rearrange("p n j -> p (n j)"))
 
-        out_1v = out_1.rearrange("(g p j) m -> g p j m", g=DG, j=4)
+        out_1v = out_1.rearrange("(g p j) m -> g j p m", g=DG, j=4)
+        out_0v = out_0.rearrange("(b p) t -> b p t", p=P)
+        stages = {}
 
-        def product_1(g, c, h, engines):
-            stage = outs.tile([P, 2, N], F32, name="stage1", tag="stage", bufs=8)
-            for i in range(2):
-                j = 2 * h + i
-                bank = psum.tile([P, N], F32, name="bank_1", tag="bank")
-                for s in range(TG):
-                    cols = slice(j * P, j * P + P)
-                    nc.tensor.matmul_mx(
-                        out=bank[:], lhsT=dt_codes[g][:, s, cols].bitcast(E5M2), lhsT_scale=dt_scales[g][:, s, cols],
-                        rhs=x_codes[c][:, s, :].bitcast(E4M3), rhs_scale=x_scales[c][:, s, :],
-                        start=(s == 0), stop=(s == TG - 1))
-                evac(engines[i], stage[:, i, :], bank[:])
-            nc.sync.dma_start(out=out_1v[g, :, 2 * h : 2 * h + 2, c * N : c * N + N], in_=stage[:])
+        def stage_tile(key, width):
+            if key not in stages:
+                stages[key] = outs.tile([P, width], F32, name="stage", tag="stage")
+            return stages[key]
 
-        out_0v = out_0.rearrange("(c b p) t -> c p b t", c=MC, p=P)
+        done = {}
 
-        def product_0(c, s, h, engines, pieces=1):
-            stage = outs.tile([P, 2, N], F32, name="stage0", tag="stage", bufs=8)
-            toks = slice(s * N, s * N + N)
-            for i in range(2):
-                b = 2 * h + i
-                cols = slice(b * P, b * P + P)
-                bank = psum.tile([P, N], F32, name="bank_0", tag="bank")
-                for g in range(DG):
-                    nc.tensor.matmul_mx(
-                        out=bank[:], lhsT=v_codes[c][:, g, cols].bitcast(E4M3), lhsT_scale=v_scales[c][:, g, cols],
-                        rhs=d_codes[s][:, g, :].bitcast(E5M2), rhs_scale=d_scales[s][:, g, :],
-                        start=(g == 0), stop=(g == DG - 1))
-                evac(engines[i], stage[:, i, :].rearrange("p (q u e) -> p q u e", u=2, e=2),
-                     bank[:].rearrange("p (u q e) -> p q u e", u=2, e=2))
-                if pieces == 2:
-                    nc.sync.dma_start(out=out_0v[c, :, b, toks], in_=stage[:, i, :])
-            if pieces == 1:
-                nc.sync.dma_start(out=out_0v[c, :, 2 * h : 2 * h + 2, toks], in_=stage[:])
+        def product_1(g, j, c, engine):
+            stage = stage_tile((1, g, j), M)
+            bank = psum.tile([P, N], F32, name="bank_1", tag="bank")
+            cols = slice(j * P, j * P + P)
+            for s in range(TG):
+                nc.tensor.matmul_mx(
+                    out=bank[:], lhsT=dt_codes[g][:, s, cols].bitcast(E5M2), lhsT_scale=dt_scales[g][:, s, cols],
+                    rhs=x_codes[c][:, s, :].bitcast(E4M3), rhs_scale=x_scales[c][:, s, :],
+                    start=(s == 0), stop=(s == TG - 1))
+            evac(engine, stage[:, c * N : c * N + N], bank[:])
+            done[1, g, j] = done.get((1, g, j), 0) + 1
+            if done[1, g, j] == MC:
+                nc.sync.dma_start(out=out_1v[g, j], in_=stage[:])
 
-        absolute(0, 0)
+        def product_0(b, s, engine):
+            stage = stage_tile((0, b), T)
+            c, cols, toks = b // 4, slice((b % 4) * P, (b % 4) * P + P), slice(s * N, s * N + N)
+            bank = psum.tile([P, N], F32, name="bank_0", tag="bank")
+            for g in range(DG):
+                nc.tensor.matmul_mx(
+                    out=bank[:], lhsT=v_codes[c][:, g, cols].bitcast(E4M3), lhsT_scale=v_scales[c][:, g, cols],
+                    rhs=d_codes[s][:, g, :].bitcast(E5M2), rhs_scale=d_scales[s][:, g, :],
+                    start=(g == 0), stop=(g == DG - 1))
+            evac(engine, stage[:, toks].rearrange("p (q u e) -> p q u e", u=2, e=2),
+                 bank[:].rearrange("p (u q e) -> p q u e", u=2, e=2))
+            done[0, b] = done.get((0, b), 0) + 1
+            if b == 4 * MC - 1:
+                nc.sync.dma_start(out=out_0v[b, :, toks], in_=stage[:, toks])
+            elif done[0, b] == TG:
+                nc.sync.dma_start(out=out_0v[b], in_=stage[:])
+
+        absolute(0, 0, "S")
+        absolute(0, 1, "V")
         mask(0, 0)
-        absolute(0, 1)
-        absolute(0, 2)
         mask(0, 1)
-        absolute(0, 3)
-        transpose_d(0, 0, "SSV")
-        mask(0, 2)
-        mask(0, 3)
-        transpose_x(0, "SVS")
+        transpose_x(0, "SSS")
+        absolute(0, 2, "V")
         transpose_x(1, "SVS")
-        group_d(0, 0)
-        transpose_d(0, 1, "SVS")
+        mask(0, 2)
+        absolute(0, 3, "V")
+        mask(0, 3)
+        transpose_d(0, 0, "SSS")
         quantize_x(0, 0)
         quantize_x(0, 1)
         quantize_x(0, 2)
-        transpose_x(2, "SVS")
-        quantize_dt(0, 0)
-        quantize_dt(0, 1)
-        quantize_dt(0, 2)
-        transpose_x(3, "SSS")
+        transpose_d(0, 1, "SSS")
+        quantize_dt(0, 0, 0)
+        quantize_dt(0, 1, 0)
+        quantize_dt(0, 2, 0)
+        quantize_dt(0, 0, 1)
+        quantize_dt(0, 1, 1)
+        quantize_dt(0, 2, 1)
+        transpose_x(2, "SSS")
+        group_d(0, 0)
+        transpose_x(3, "SVS")
+        quantize_d(0, 0)
+        transpose_x(4, "SSS")
         quantize_x(1, 0)
-        transpose_x(4, "SVS")
         quantize_x(1, 1)
         quantize_x(1, 2)
         transpose_x(5, "SVS")
-        absolute(1, 0)
+        absolute(1, 0, "S")
         quantize_x(2, 0)
         quantize_x(2, 1)
         quantize_x(2, 2)
-        product_1(0, 0, 0, "SS")
-        absolute(1, 1)
-        mask(1, 0)
-        product_1(0, 0, 1, "SS")
-        mask(1, 1)
-        product_1(0, 1, 0, "SV")
-        absolute(1, 2)
-        quantize_d(0, 0)
-        product_1(0, 1, 1, "SS")
-        mask(1, 2)
-        absolute(1, 3)
-        transpose_d(1, 0, "SVS")
-        product_1(0, 2, 0, "SS")
-        mask(1, 3)
-        transpose_d(1, 1, "SVS")
-        group_d(1, 0)
-        quantize_dt(1, 0)
-        quantize_dt(1, 1)
-        quantize_dt(1, 2)
-        product_1(0, 2, 1, "SS")
-        group_v(0, 0)
-        quantize_d(1, 0)
-        product_1(1, 0, 0, "SS")
-        quantize_v(0, 0)
-        group_v(1, 0)
-        product_1(1, 0, 1, "SS")
-        quantize_v(1, 0)
+        product_1(0, 0, 0, "S")
+        product_1(0, 1, 0, "S")
+        absolute(1, 1, "S")
         group_d(0, 1)
-        product_1(1, 1, 0, "SS")
-        group_d(1, 1)
+        product_1(0, 2, 0, "S")
+        product_1(0, 3, 0, "S")
+        mask(1, 0)
         quantize_d(0, 1)
-        product_0(0, 0, 0, "SS", 1)
-        product_0(0, 0, 1, "SS", 1)
-        product_1(1, 1, 1, "SS")
+        absolute(1, 2, "S")
+        product_1(0, 0, 1, "S")
+        product_1(0, 1, 1, "V")
+        mask(1, 1)
+        product_1(0, 2, 1, "S")
+        product_1(0, 3, 1, "S")
+        mask(1, 2)
+        transpose_d(1, 0, "SSS")
+        absolute(1, 3, "V")
+        product_1(0, 0, 2, "S")
+        product_1(0, 1, 2, "V")
+        quantize_dt(1, 0, 0)
+        quantize_dt(1, 1, 0)
+        quantize_dt(1, 2, 0)
+        mask(1, 3)
+        product_1(0, 2, 2, "S")
+        product_1(0, 3, 2, "S")
+        group_v(0, 0)
+        product_1(1, 0, 0, "S")
+        product_1(1, 0, 1, "S")
+        product_1(1, 0, 2, "S")
+        transpose_d(1, 1, "SSS")
+        group_d(1, 0)
+        quantize_v(0, 0)
+        product_1(1, 1, 0, "S")
+        product_1(1, 1, 1, "S")
+        product_1(1, 1, 2, "S")
+        quantize_dt(1, 0, 1)
+        quantize_dt(1, 1, 1)
+        quantize_dt(1, 2, 1)
+        group_v(1, 0)
+        quantize_d(1, 0)
+        group_d(1, 2)
+        quantize_v(1, 0)
+        product_1(1, 2, 0, "S")
+        product_1(1, 2, 1, "S")
+        product_1(1, 2, 2, "S")
+        group_d(1, 1)
+        quantize_d(1, 2)
+        group_d(0, 2)
         quantize_d(1, 1)
+        product_1(1, 3, 0, "S")
+        product_1(1, 3, 1, "S")
+        product_1(1, 3, 2, "S")
+        quantize_d(0, 2)
         group_v(0, 1)
-        product_1(1, 2, 0, "SS")
-        product_0(0, 1, 0, "SS", 1)
+        product_0(0, 0, "S")
+        product_0(0, 1, "S")
+        product_0(0, 2, "S")
+        product_0(1, 0, "S")
+        product_0(1, 1, "S")
+        product_0(1, 2, "S")
         group_v(1, 1)
         quantize_v(0, 1)
-        product_0(0, 1, 1, "SS", 1)
-        product_1(1, 2, 1, "SS")
-        group_d(0, 2)
+        product_0(2, 0, "S")
+        product_0(2, 1, "S")
+        product_0(2, 2, "S")
+        product_0(3, 0, "S")
+        product_0(3, 1, "S")
+        product_0(3, 2, "S")
         quantize_v(1, 1)
-        group_d(1, 2)
-        quantize_d(0, 2)
-        product_0(1, 0, 0, "SS", 1)
-        quantize_d(1, 2)
         group_v(0, 2)
-        product_0(1, 0, 1, "SS", 1)
         group_v(1, 2)
         quantize_v(0, 2)
-        product_0(1, 1, 0, "SS", 1)
+        product_0(4, 0, "S")
+        product_0(4, 1, "S")
+        product_0(4, 2, "S")
         quantize_v(1, 2)
-        product_0(1, 1, 1, "SV", 1)
-        product_0(0, 2, 0, "SV", 1)
-        product_0(0, 2, 1, "SV", 1)
-        product_0(1, 2, 0, "SV", 1)
-        product_0(1, 2, 1, "SV", 1)
-        product_0(2, 0, 0, "SV", 1)
-        product_0(2, 0, 1, "SV", 1)
-        product_0(2, 1, 0, "SV", 1)
-        product_0(2, 1, 1, "SV", 1)
-        product_0(2, 2, 0, "SV", 1)
-        product_0(2, 2, 1, "SV", 2)
+        product_0(5, 0, "S")
+        product_0(5, 1, "V")
+        product_0(5, 2, "S")
+        product_0(6, 0, "S")
+        product_0(6, 1, "V")
+        product_0(6, 2, "S")
+        product_0(7, 0, "S")
+        product_0(7, 1, "V")
+        product_0(7, 2, "S")
+        product_0(8, 0, "V")
+        product_0(8, 1, "S")
+        product_0(8, 2, "V")
+        product_0(9, 0, "S")
+        product_0(9, 1, "V")
+        product_0(9, 2, "S")
+        product_0(10, 0, "V")
+        product_0(10, 1, "S")
+        product_0(10, 2, "V")
+        product_0(11, 0, "S")
+        product_0(11, 1, "V")
+        product_0(11, 2, "S")

@@ -33,13 +33,22 @@ def tile_blueboxlayer_pb_v_kernel(tc, Z, X, U, V, l1, mat, grad_out, out_0, out_
         keep = ctx.enter_context(tc.tile_pool(name="keep", bufs=1))
         work = ctx.enter_context(tc.tile_pool(name="work", bufs=3))
         outs = ctx.enter_context(tc.tile_pool(name="outs", bufs=7))
-        psum = ctx.enter_context(tc.psum_pool(name="psum", bufs=8))
+        psum = ctx.enter_context(tc.psum_pool(name="psum", bufs=7))
+        junk = ctx.enter_context(tc.psum_pool(name="junk", bufs=1))
         ctx.enter_context(tc.manual_schedule())
 
         thres = const.tile([P, 1], BF16, name="thres")
         nc.scalar.dma_start(out=thres[:], in_=l1.partition_broadcast(P))
         ident = const.tile([P, P], F32, name="ident")
         make_identity(nc, ident[:])
+        ones = const.tile([P, N], BF16, name="ones", align_bytes=64)
+        nc.vector.memset(ones[:], 1.0)
+        junk_bank = junk.tile([P, N], F32, name="junk_bank")
+
+        def keep_warm(count, when):
+            rhs = ones[:] if when == 0 else grads[0][:, 0, 0:N] if when == 1 else dmat[0][:, when - 2, 0:N]
+            for k in range(count):
+                nc.tensor.matmul(junk_bank[:], lhsT=ones[:, 0:P], rhs=rhs, start=True, stop=True)
 
         mat_v = mat.rearrange("(g p j) t -> g p j t", g=DG, j=4)
         grad_v = grad_out.rearrange("(g p j) t -> g p j t", g=DG, j=4)
@@ -77,8 +86,10 @@ def tile_blueboxlayer_pb_v_kernel(tc, Z, X, U, V, l1, mat, grad_out, out_0, out_
         load_mat(0, 2)
         load_grad(0, 1)
         load_mat(0, 3)
-        load_x(2, 2)
-        load_x(4, 2)
+        load_x(2)
+        load_x(3)
+        load_x(4)
+        load_x(5)
         load_mat(1, 0, 2)
         load_grad(1, 0, 2)
         load_mat(1, 2, 2)
@@ -224,70 +235,76 @@ def tile_blueboxlayer_pb_v_kernel(tc, Z, X, U, V, l1, mat, grad_out, out_0, out_
             elif done[0, b] == TG:
                 nc.sync.dma_start(out=out_0v[b], in_=stage[:])
 
+        keep_warm(7, 1)
         absolute(0, 0, "S")
         absolute(0, 1, "V")
         mask(0, 0)
+        keep_warm(5, 0)
         mask(0, 1)
         transpose_x(0, "SSS")
         absolute(0, 2, "V")
-        transpose_x(1, "SVS")
-        mask(0, 2)
-        absolute(0, 3, "V")
-        mask(0, 3)
-        transpose_d(0, 0, "SSS")
-        quantize_x(0, 0)
-        quantize_x(0, 1)
-        quantize_x(0, 2)
-        transpose_d(0, 1, "SSS")
+        keep_warm(2, 0)
+        transpose_d(0, 0, "SVS")
+        transpose_x(1, "SSS")
         quantize_dt(0, 0, 0)
         quantize_dt(0, 1, 0)
         quantize_dt(0, 2, 0)
-        quantize_dt(0, 0, 1)
-        quantize_dt(0, 1, 1)
-        quantize_dt(0, 2, 1)
-        transpose_x(2, "SSS")
+        keep_warm(7, 0)
+        quantize_x(0, 0)
+        quantize_x(0, 1)
+        quantize_x(0, 2)
+        absolute(0, 3, "S")
+        mask(0, 2)
+        product_1(0, 0, 0, "S")
+        mask(0, 3)
+        transpose_x(2, "SVS")
+        keep_warm(2, 0)
+        transpose_x(3, "SSS")
         group_d(0, 0)
-        transpose_x(3, "SVS")
-        quantize_d(0, 0)
-        transpose_x(4, "SSS")
+        product_1(0, 1, 0, "S")
+        transpose_d(0, 1, "SVS")
         quantize_x(1, 0)
         quantize_x(1, 1)
         quantize_x(1, 2)
-        transpose_x(5, "SVS")
-        absolute(1, 0, "S")
+        quantize_d(0, 0)
+        keep_warm(1, 0)
+        transpose_x(4, "SSS")
+        absolute(1, 0, "V")
+        absolute(1, 1, "V")
+        quantize_dt(0, 0, 1)
+        quantize_dt(0, 1, 1)
+        quantize_dt(0, 2, 1)
+        product_1(0, 1, 1, "S")
+        transpose_x(5, "SSS")
+        mask(1, 0)
         quantize_x(2, 0)
         quantize_x(2, 1)
         quantize_x(2, 2)
-        product_1(0, 0, 0, "S")
-        product_1(0, 1, 0, "S")
-        absolute(1, 1, "S")
-        group_d(0, 1)
+        product_1(0, 0, 1, "S")
         product_1(0, 2, 0, "S")
         product_1(0, 3, 0, "S")
-        mask(1, 0)
-        quantize_d(0, 1)
-        absolute(1, 2, "S")
-        product_1(0, 0, 1, "S")
-        product_1(0, 1, 1, "V")
         mask(1, 1)
         product_1(0, 2, 1, "S")
+        absolute(1, 2, "S")
         product_1(0, 3, 1, "S")
-        mask(1, 2)
-        transpose_d(1, 0, "SSS")
         absolute(1, 3, "V")
+        mask(1, 2)
         product_1(0, 0, 2, "S")
-        product_1(0, 1, 2, "V")
+        product_1(0, 1, 2, "S")
+        mask(1, 3)
+        transpose_d(1, 0, "SSS")
         quantize_dt(1, 0, 0)
         quantize_dt(1, 1, 0)
         quantize_dt(1, 2, 0)
-        mask(1, 3)
         product_1(0, 2, 2, "S")
+        group_d(0, 1)
+        transpose_d(1, 1, "SSS")
         product_1(0, 3, 2, "S")
         group_v(0, 0)
         product_1(1, 0, 0, "S")
         product_1(1, 0, 1, "S")
         product_1(1, 0, 2, "S")
-        transpose_d(1, 1, "SSS")
+        quantize_d(0, 1)
         group_d(1, 0)
         quantize_v(0, 0)
         product_1(1, 1, 0, "S")

@@ -33,28 +33,21 @@ def tile_blueboxlayer_pb_v_kernel(tc, Z, X, U, V, l1, mat, grad_out, out_0, out_
         keep = ctx.enter_context(tc.tile_pool(name="keep", bufs=1))
         work = ctx.enter_context(tc.tile_pool(name="work", bufs=3))
         outs = ctx.enter_context(tc.tile_pool(name="outs", bufs=7))
-        psum = ctx.enter_context(tc.psum_pool(name="psum", bufs=7))
-        junk = ctx.enter_context(tc.psum_pool(name="junk", bufs=1))
+        psum = ctx.enter_context(tc.psum_pool(name="psum", bufs=8))
         ctx.enter_context(tc.manual_schedule())
 
         thres = const.tile([P, 1], BF16, name="thres")
         nc.scalar.dma_start(out=thres[:], in_=l1.partition_broadcast(P))
         ident = const.tile([P, P], F32, name="ident")
         make_identity(nc, ident[:])
-        ones = const.tile([P, N], BF16, name="ones", align_bytes=64)
-        nc.vector.memset(ones[:], 1.0)
-        junk_bank = junk.tile([P, N], F32, name="junk_bank")
-
-        def keep_warm(count, when):
-            rhs = ones[:] if when == 0 else grads[0][:, 0, 0:N] if when == 1 else dmat[0][:, when - 2, 0:N]
-            for k in range(count):
-                nc.tensor.matmul(junk_bank[:], lhsT=ones[:, 0:P], rhs=rhs, start=True, stop=True)
 
         mat_v = mat.rearrange("(g p j) t -> g p j t", g=DG, j=4)
         grad_v = grad_out.rearrange("(g p j) t -> g p j t", g=DG, j=4)
         v_v = V.rearrange("(g p j) m -> g p j m", g=DG, j=4)
         x_v = X.rearrange("(c p i) t -> c p i t", c=MC, i=4)
-        mats, grads, xs, vs = {}, {}, {}, {}
+        mats, xs, vs = {}, {}, {}
+        grads = [keep.tile([P, 4, T], BF16, name="grad%d" % g, align_bytes=64) for g in range(DG)]
+        dmat = grads
 
         def raw_tile(store, key, shape, dtype):
             if key not in store:
@@ -66,8 +59,7 @@ def tile_blueboxlayer_pb_v_kernel(tc, Z, X, U, V, l1, mat, grad_out, out_0, out_
             nc.sync.dma_start(out=t[:, j % 2 : j % 2 + n, :], in_=mat_v[g, :, j : j + n, :])
 
         def load_grad(g, h, n=1):
-            t = raw_tile(grads, g, [P, 4, T], BF16)
-            nc.sync.dma_start(out=t[:, 2 * h : 2 * h + 2 * n, :], in_=grad_v[g, :, 2 * h : 2 * h + 2 * n, :])
+            nc.sync.dma_start(out=grads[g][:, 2 * h : 2 * h + 2 * n, :], in_=grad_v[g, :, 2 * h : 2 * h + 2 * n, :])
 
         def load_x(b, n=1):
             t = raw_tile(xs, b // 2, [P, 4, T], BF16)
@@ -95,7 +87,6 @@ def tile_blueboxlayer_pb_v_kernel(tc, Z, X, U, V, l1, mat, grad_out, out_0, out_
         load_mat(1, 2, 2)
         load_v(0)
         load_v(1)
-        dmat = [keep.tile([P, 4, T], BF16, name="dmat%d" % g, align_bytes=64) for g in range(DG)]
         dt_codes = [keep.tile([P, TG, K], U32, name="dt_codes%d" % g, align_bytes=64) for g in range(DG)]
         dt_scales = [keep.tile([P, TG, K], U8, name="dt_scales%d" % g, align_bytes=64) for g in range(DG)]
         x_codes = [keep.tile([P, TG, N], U32, name="x_codes%d" % c, align_bytes=64) for c in range(MC)]
@@ -120,13 +111,9 @@ def tile_blueboxlayer_pb_v_kernel(tc, Z, X, U, V, l1, mat, grad_out, out_0, out_
                 nc.vector.tensor_scalar(out=bits, in0=bits, scalar1=0x7FFFFFFF, scalar2=None, op0=ALU.bitwise_and)
 
         def mask(g, j):
-            for u in range(2):
-                nc.vector.scalar_tensor_tensor(
-                    out=dmat[g][:, j, :].rearrange("p (s u q e) -> p s u q e", s=TG, u=2, e=2)[:, :, u],
-                    in0=mats[g, j // 2][:, j % 2, :].rearrange("p (s q u e) -> p s q u e", s=TG, u=2, e=2)[:, :, :, u],
-                    scalar=thres[:, 0:1],
-                    in1=grads[g][:, j, :].rearrange("p (s q u e) -> p s q u e", s=TG, u=2, e=2)[:, :, :, u],
-                    op0=ALU.is_gt, op1=ALU.mult)
+            nc.vector.scalar_tensor_tensor(
+                out=dmat[g][:, j, :], in0=mats[g, j // 2][:, j % 2, :], scalar=thres[:, 0:1],
+                in1=grads[g][:, j, :], op0=ALU.is_gt, op1=ALU.mult)
 
         dt_rows, x_rows = {}, {}
 
@@ -141,8 +128,8 @@ def tile_blueboxlayer_pb_v_kernel(tc, Z, X, U, V, l1, mat, grad_out, out_0, out_
                 bank = psum.tile([P, 4, P], F32, name="bank_t", tag="bank")
                 for i in range(2):
                     for u in range(2):
-                        first = i * (T // 2) + 256 * s + 128 * u
-                        nc.tensor.transpose(bank[:, 2 * i + u, :], words[:, first : first + 128], ident[:])
+                        first = i * (T // 2) + 256 * s + u
+                        nc.tensor.transpose(bank[:, 2 * i + u, :], words[:, first : first + 255 : 2], ident[:])
                 evac(engines[s],
                      dt_rows[g, s][:].bitcast(F32).rearrange("q (i p u) -> q i p u", i=4, u=2)[:, 2 * h : 2 * h + 2],
                      bank[:].rearrange("q (i u) p -> q i p u", u=2))
@@ -227,83 +214,76 @@ def tile_blueboxlayer_pb_v_kernel(tc, Z, X, U, V, l1, mat, grad_out, out_0, out_
                     out=bank[:], lhsT=v_codes[c][:, g, cols].bitcast(E4M3), lhsT_scale=v_scales[c][:, g, cols],
                     rhs=d_codes[s][:, g, :].bitcast(E5M2), rhs_scale=d_scales[s][:, g, :],
                     start=(g == 0), stop=(g == DG - 1))
-            evac(engine, stage[:, toks].rearrange("p (q u e) -> p q u e", u=2, e=2),
-                 bank[:].rearrange("p (u q e) -> p q u e", u=2, e=2))
+            evac(engine, stage[:, toks], bank[:])
             done[0, b] = done.get((0, b), 0) + 1
             if b == 4 * MC - 1:
                 nc.sync.dma_start(out=out_0v[b, :, toks], in_=stage[:, toks])
             elif done[0, b] == TG:
                 nc.sync.dma_start(out=out_0v[b], in_=stage[:])
 
-        keep_warm(7, 1)
-        absolute(0, 0, "S")
-        absolute(0, 1, "V")
+        absolute(0, 0, "V")
         mask(0, 0)
-        keep_warm(5, 0)
+        absolute(0, 1, "S")
         mask(0, 1)
         transpose_x(0, "SSS")
-        absolute(0, 2, "V")
-        keep_warm(2, 0)
-        transpose_d(0, 0, "SVS")
-        transpose_x(1, "SSS")
-        quantize_dt(0, 0, 0)
-        quantize_dt(0, 1, 0)
-        quantize_dt(0, 2, 0)
-        keep_warm(7, 0)
+        absolute(0, 2, "S")
+        transpose_d(0, 0, "VVV")
+        transpose_x(1, "SVS")
         quantize_x(0, 0)
         quantize_x(0, 1)
         quantize_x(0, 2)
+        quantize_dt(0, 0, 0)
+        quantize_dt(0, 1, 0)
+        quantize_dt(0, 2, 0)
         absolute(0, 3, "S")
         mask(0, 2)
-        product_1(0, 0, 0, "S")
         mask(0, 3)
+        product_1(0, 0, 0, "S")
         transpose_x(2, "SVS")
-        keep_warm(2, 0)
-        transpose_x(3, "SSS")
         group_d(0, 0)
-        product_1(0, 1, 0, "S")
-        transpose_d(0, 1, "SVS")
+        transpose_x(3, "SSS")
+        transpose_d(0, 1, "SSS")
         quantize_x(1, 0)
         quantize_x(1, 1)
         quantize_x(1, 2)
-        quantize_d(0, 0)
-        keep_warm(1, 0)
         transpose_x(4, "SSS")
-        absolute(1, 0, "V")
-        absolute(1, 1, "V")
         quantize_dt(0, 0, 1)
         quantize_dt(0, 1, 1)
         quantize_dt(0, 2, 1)
-        product_1(0, 1, 1, "S")
         transpose_x(5, "SSS")
-        mask(1, 0)
+        quantize_d(0, 0)
+        absolute(1, 0, "S")
         quantize_x(2, 0)
         quantize_x(2, 1)
         quantize_x(2, 2)
-        product_1(0, 0, 1, "S")
+        product_1(0, 1, 0, "S")
         product_1(0, 2, 0, "S")
         product_1(0, 3, 0, "S")
-        mask(1, 1)
+        product_1(0, 0, 1, "S")
+        product_1(0, 1, 1, "S")
+        absolute(1, 1, "V")
+        mask(1, 0)
         product_1(0, 2, 1, "S")
-        absolute(1, 2, "S")
+        mask(1, 1)
         product_1(0, 3, 1, "S")
-        absolute(1, 3, "V")
-        mask(1, 2)
         product_1(0, 0, 2, "S")
-        product_1(0, 1, 2, "S")
-        mask(1, 3)
+        absolute(1, 2, "V")
         transpose_d(1, 0, "SSS")
+        mask(1, 2)
+        absolute(1, 3, "V")
+        product_1(0, 1, 2, "S")
         quantize_dt(1, 0, 0)
         quantize_dt(1, 1, 0)
         quantize_dt(1, 2, 0)
         product_1(0, 2, 2, "S")
-        group_d(0, 1)
-        transpose_d(1, 1, "SSS")
+        mask(1, 3)
         product_1(0, 3, 2, "S")
+        group_d(0, 1)
         group_v(0, 0)
         product_1(1, 0, 0, "S")
         product_1(1, 0, 1, "S")
         product_1(1, 0, 2, "S")
+        transpose_d(1, 1, "SSS")
         quantize_d(0, 1)
         group_d(1, 0)
         quantize_v(0, 0)
@@ -313,27 +293,27 @@ def tile_blueboxlayer_pb_v_kernel(tc, Z, X, U, V, l1, mat, grad_out, out_0, out_
         quantize_dt(1, 0, 1)
         quantize_dt(1, 1, 1)
         quantize_dt(1, 2, 1)
-        group_v(1, 0)
         quantize_d(1, 0)
-        group_d(1, 2)
+        group_v(1, 0)
+        group_d(0, 2)
         quantize_v(1, 0)
         product_1(1, 2, 0, "S")
         product_1(1, 2, 1, "S")
         product_1(1, 2, 2, "S")
         group_d(1, 1)
-        quantize_d(1, 2)
-        group_d(0, 2)
+        quantize_d(0, 2)
+        group_d(1, 2)
         quantize_d(1, 1)
         product_1(1, 3, 0, "S")
         product_1(1, 3, 1, "S")
         product_1(1, 3, 2, "S")
-        quantize_d(0, 2)
+        quantize_d(1, 2)
         group_v(0, 1)
         product_0(0, 0, "S")
-        product_0(0, 1, "S")
-        product_0(0, 2, "S")
         product_0(1, 0, "S")
+        product_0(0, 1, "S")
         product_0(1, 1, "S")
+        product_0(0, 2, "S")
         product_0(1, 2, "S")
         group_v(1, 1)
         quantize_v(0, 1)

@@ -80,8 +80,7 @@ def tile_blueboxlayer_pb_v_kernel(tc, Z, X, U, V, l1, mat, grad_out, out_0, out_
         load_mat(0, 3)
         load_x(2)
         load_x(3)
-        load_x(4)
-        load_x(5)
+        load_x(4, 2)
         load_mat(1, 0, 2)
         load_grad(1, 0, 2)
         load_mat(1, 2, 2)
@@ -221,116 +220,116 @@ def tile_blueboxlayer_pb_v_kernel(tc, Z, X, U, V, l1, mat, grad_out, out_0, out_
             elif done[0, b] == TG:
                 nc.sync.dma_start(out=out_0v[b], in_=stage[:])
 
-        absolute(0, 0, "V")
+        absolute(0, 0, "S")
         mask(0, 0)
         absolute(0, 1, "S")
         mask(0, 1)
-        transpose_x(0, "SSS")
-        absolute(0, 2, "S")
-        transpose_d(0, 0, "VVV")
-        transpose_x(1, "SVS")
-        quantize_x(0, 0)
-        quantize_x(0, 1)
-        quantize_x(0, 2)
+        transpose_x(0, "SVS")
+        transpose_d(0, 0, "SVV")
+        transpose_x(1, "VSS")
         quantize_dt(0, 0, 0)
         quantize_dt(0, 1, 0)
         quantize_dt(0, 2, 0)
+        quantize_x(0, 0)
+        quantize_x(0, 1)
+        quantize_x(0, 2)
+        absolute(0, 2, "V")
         absolute(0, 3, "S")
         mask(0, 2)
-        mask(0, 3)
         product_1(0, 0, 0, "S")
-        transpose_x(2, "SVS")
+        mask(0, 3)
         group_d(0, 0)
+        transpose_x(2, "VSS")
         transpose_x(3, "SSS")
+        group_d(0, 1)
         transpose_d(0, 1, "SSS")
         quantize_x(1, 0)
         quantize_x(1, 1)
         quantize_x(1, 2)
-        transpose_x(4, "SSS")
+        transpose_x(4, "VSS")
         quantize_dt(0, 0, 1)
         quantize_dt(0, 1, 1)
         quantize_dt(0, 2, 1)
         transpose_x(5, "SSS")
         quantize_d(0, 0)
         absolute(1, 0, "S")
-        quantize_x(2, 0)
-        quantize_x(2, 1)
-        quantize_x(2, 2)
+        absolute(1, 1, "S")
         product_1(0, 1, 0, "S")
         product_1(0, 2, 0, "S")
         product_1(0, 3, 0, "S")
+        quantize_x(2, 0)
+        quantize_x(2, 1)
+        quantize_x(2, 2)
+        quantize_d(0, 1)
         product_1(0, 0, 1, "S")
-        product_1(0, 1, 1, "S")
-        absolute(1, 1, "V")
         mask(1, 0)
+        product_1(0, 1, 1, "S")
         product_1(0, 2, 1, "S")
-        mask(1, 1)
         product_1(0, 3, 1, "S")
+        mask(1, 1)
         product_1(0, 0, 2, "S")
-        absolute(1, 2, "V")
         transpose_d(1, 0, "SSS")
+        absolute(1, 2, "V")
         mask(1, 2)
-        absolute(1, 3, "V")
         product_1(0, 1, 2, "S")
         quantize_dt(1, 0, 0)
         quantize_dt(1, 1, 0)
         quantize_dt(1, 2, 0)
         product_1(0, 2, 2, "S")
-        mask(1, 3)
         product_1(0, 3, 2, "S")
-        group_d(0, 1)
-        group_v(0, 0)
+        absolute(1, 3, "V")
         product_1(1, 0, 0, "S")
         product_1(1, 0, 1, "S")
         product_1(1, 0, 2, "S")
+        mask(1, 3)
+        group_v(0, 0)
+        group_d(0, 2)
         transpose_d(1, 1, "SSS")
-        quantize_d(0, 1)
-        group_d(1, 0)
-        quantize_v(0, 0)
         product_1(1, 1, 0, "S")
         product_1(1, 1, 1, "S")
         product_1(1, 1, 2, "S")
         quantize_dt(1, 0, 1)
         quantize_dt(1, 1, 1)
         quantize_dt(1, 2, 1)
-        quantize_d(1, 0)
+        quantize_v(0, 0)
+        quantize_d(0, 2)
+        group_d(1, 0)
         group_v(1, 0)
-        group_d(0, 2)
-        quantize_v(1, 0)
+        quantize_d(1, 0)
         product_1(1, 2, 0, "S")
         product_1(1, 2, 1, "S")
         product_1(1, 2, 2, "S")
         group_d(1, 1)
-        quantize_d(0, 2)
-        group_d(1, 2)
+        quantize_v(1, 0)
         quantize_d(1, 1)
         product_1(1, 3, 0, "S")
         product_1(1, 3, 1, "S")
         product_1(1, 3, 2, "S")
+        group_d(1, 2)
         quantize_d(1, 2)
-        group_v(0, 1)
         product_0(0, 0, "S")
         product_0(1, 0, "S")
         product_0(0, 1, "S")
         product_0(1, 1, "S")
         product_0(0, 2, "S")
         product_0(1, 2, "S")
+        group_v(0, 1)
         group_v(1, 1)
         quantize_v(0, 1)
         product_0(2, 0, "S")
         product_0(2, 1, "S")
         product_0(2, 2, "S")
+        quantize_v(1, 1)
+        group_v(1, 2)
         product_0(3, 0, "S")
         product_0(3, 1, "S")
         product_0(3, 2, "S")
-        quantize_v(1, 1)
         group_v(0, 2)
-        group_v(1, 2)
-        quantize_v(0, 2)
+        quantize_v(1, 2)
         product_0(4, 0, "S")
         product_0(4, 1, "S")
         product_0(4, 2, "S")
-        quantize_v(1, 2)
+        quantize_v(0, 2)
         product_0(5, 0, "S")
         product_0(5, 1, "V")
         product_0(5, 2, "S")

from contextlib import ExitStack

import concourse.mybir as mybir
from concourse.masks import make_identity

D, T, M = 1024, 1536, 1536
FLOPS = 2 * 2 * D * T * M
BYTES = 2 * (M * T + D * M + D * T) + 4 * (D * T + M * T + D * M) + 2

F32 = mybir.dt.float32
BF16 = mybir.dt.bfloat16
U32 = mybir.dt.uint32
U8 = mybir.dt.uint8
I32 = mybir.dt.int32
E4M3 = mybir.dt.float8_e4m3fn_x4
E5M2 = mybir.dt.float8_e5m2_x4
ALU = mybir.AluOpType
ABS = mybir.ActivationFunctionType.Abs

P = 128
K = 512
N = 512
DG = D // K
TG = T // K
MC = M // N


def tile_blueboxlayer_pb_v_kernel(tc, Z, X, U, V, l1, mat, grad_out, out_0, out_1):
    nc = tc.nc
    with ExitStack() as ctx:
        const = ctx.enter_context(tc.tile_pool(name="const", bufs=1))
        raw = ctx.enter_context(tc.tile_pool(name="raw", bufs=5))
        keep = ctx.enter_context(tc.tile_pool(name="keep", bufs=1))
        work = ctx.enter_context(tc.tile_pool(name="work", bufs=3))
        outs = ctx.enter_context(tc.tile_pool(name="outs", bufs=7))
        psum = ctx.enter_context(tc.psum_pool(name="psum", bufs=8))
        ctx.enter_context(tc.manual_schedule())

        thres = const.tile([P, 1], BF16, name="thres")
        nc.scalar.dma_start(out=thres[:], in_=l1.partition_broadcast(P))
        ident = const.tile([P, P], F32, name="ident")
        make_identity(nc, ident[:])

        mat_v = mat.rearrange("(g p j) t -> g p j t", g=DG, j=4)
        grad_v = grad_out.rearrange("(g p j) t -> g p j t", g=DG, j=4)
        v_v = V.rearrange("(g p j) m -> g p j m", g=DG, j=4)
        x_v = X.rearrange("(c p i) t -> c p i t", c=MC, i=4)
        mats, xs, vs = {}, {}, {}
        grads = [keep.tile([P, 4, T], BF16, name="grad%d" % g, align_bytes=64) for g in range(DG)]
        dmat = grads

        def raw_tile(store, key, shape, dtype):
            if key not in store:
                store[key] = raw.tile(shape, dtype, name="raw_tile", tag="raw", align_bytes=64)
            return store[key]

        def load_mat(g, j, n=1):
            t = raw_tile(mats, (g, j // 2), [P, 2, T], F32)
            nc.sync.dma_start(out=t[:, j % 2 : j % 2 + n, :], in_=mat_v[g, :, j : j + n, :])

        def load_grad(g, h, n=1):
            nc.sync.dma_start(out=grads[g][:, 2 * h : 2 * h + 2 * n, :], in_=grad_v[g, :, 2 * h : 2 * h + 2 * n, :])

        def load_x(b, n=1):
            t = raw_tile(xs, b // 2, [P, 4, T], BF16)
            i = 2 * (b % 2)
            nc.sync.dma_start(out=t[:, i : i + 2 * n, :], in_=x_v[b // 2, :, i : i + 2 * n, :])

        def load_v(g):
            t = raw_tile(vs, g, [P, 4, M], BF16)
            nc.sync.dma_start(out=t[:], in_=v_v[g])

        load_mat(0, 0)
        load_grad(0, 0)
        load_mat(0, 1)
        load_x(0)
        load_x(1)
        load_mat(0, 2)
        load_grad(0, 1)
        load_mat(0, 3)
        load_x(2)
        load_x(3)
        load_x(4, 2)
        load_mat(1, 0, 2)
        load_grad(1, 0, 2)
        load_mat(1, 2, 2)
        load_v(0)
        load_v(1)
        dt_codes = [keep.tile([P, TG, K], U32, name="dt_codes%d" % g, align_bytes=64) for g in range(DG)]
        dt_scales = [keep.tile([P, TG, K], U8, name="dt_scales%d" % g, align_bytes=64) for g in range(DG)]
        x_codes = [keep.tile([P, TG, N], U32, name="x_codes%d" % c, align_bytes=64) for c in range(MC)]
        x_scales = [keep.tile([P, TG, N], U8, name="x_scales%d" % c, align_bytes=64) for c in range(MC)]
        d_codes = [keep.tile([P, DG, N], U32, name="d_codes%d" % s, align_bytes=64) for s in range(TG)]
        d_scales = [keep.tile([P, DG, N], U8, name="d_scales%d" % s, align_bytes=64) for s in range(TG)]
        v_codes = [keep.tile([P, DG, N], U32, name="v_codes%d" % c, align_bytes=64) for c in range(MC)]
        v_scales = [keep.tile([P, DG, N], U8, name="v_scales%d" % c, align_bytes=64) for c in range(MC)]

        def evac(engine, out, in_):
            if engine == "S":
                nc.scalar.copy(out=out, in_=in_)
            else:
                nc.vector.tensor_copy(out=out, in_=in_)

        def absolute(g, j, engine):
            row = mats[g, j // 2][:, j % 2, :]
            if engine == "S":
                nc.scalar.activation(out=row, in_=row, func=ABS)
            else:
                bits = row.bitcast(I32)
                nc.vector.tensor_scalar(out=bits, in0=bits, scalar1=0x7FFFFFFF, scalar2=None, op0=ALU.bitwise_and)

        def mask(g, j):
            nc.vector.scalar_tensor_tensor(
                out=dmat[g][:, j, :], in0=mats[g, j // 2][:, j % 2, :], scalar=thres[:, 0:1],
                in1=grads[g][:, j, :], op0=ALU.is_gt, op1=ALU.mult)

        dt_rows, x_rows = {}, {}

        def words_of(rows):
            return rows.rearrange("p i t -> p (i t)").bitcast(F32)

        def transpose_d(g, h, engines):
            words = words_of(dmat[g][:, 2 * h : 2 * h + 2, :])
            for s in range(TG):
                if h == 0:
                    dt_rows[g, s] = work.tile([P, K * 4], BF16, name="dt_rows", tag="dt_rows", align_bytes=64)
                bank = psum.tile([P, 4, P], F32, name="bank_t", tag="bank")
                for i in range(2):
                    for u in range(2):
                        first = i * (T // 2) + 256 * s + u
                        nc.tensor.transpose(bank[:, 2 * i + u, :], words[:, first : first + 255 : 2], ident[:])
                evac(engines[s],
                     dt_rows[g, s][:].bitcast(F32).rearrange("q (i p u) -> q i p u", i=4, u=2)[:, 2 * h : 2 * h + 2],
                     bank[:].rearrange("q (i u) p -> q i p u", u=2))

        def quantize_dt(g, s, h):
            half = slice(h * K // 2, (h + 1) * K // 2)
            nc.vector.quantize_mx(out=dt_codes[g][:, s, half].bitcast(E5M2), scales=dt_scales[g][:, s, half],
                                  in_=dt_rows[g, s][:, h * 2 * K : (h + 1) * 2 * K])

        def transpose_x(b, engines):
            c, h = b // 2, b % 2
            words = words_of(xs[c][:, 2 * h : 2 * h + 2, :])
            for s in range(TG):
                if h == 0:
                    x_rows[c, s] = work.tile([P, N * 4], BF16, name="x_rows", tag="x_rows", bufs=5, align_bytes=64)
                bank = psum.tile([P, 4, P], F32, name="bank_t", tag="bank")
                for i in range(2):
                    for u in range(2):
                        first = i * (T // 2) + 256 * s + u
                        nc.tensor.transpose(bank[:, 2 * i + u, :], words[:, first : first + 255 : 2], ident[:])
                evac(engines[s],
                     x_rows[c, s][:].bitcast(F32).rearrange("q (p h w) -> q p h w", h=2, w=4)[:, :, h],
                     bank[:].rearrange("q w p -> q p w"))

        def quantize_x(c, s):
            nc.vector.quantize_mx(out=x_codes[c][:, s, :].bitcast(E4M3), scales=x_scales[c][:, s, :], in_=x_rows[c, s][:])

        grouped = {}

        def group(key, src, cols):
            t = work.tile([P, N, 4], BF16, name="grouped", tag="grouped", bufs=2, align_bytes=64)
            nc.vector.tensor_copy(
                out=t[:].rearrange("p (c i) j -> p c j i", i=4),
                in_=src[:, :, cols].rearrange("p j (c i) -> p c j i", i=4))
            grouped[key] = t

        def group_d(g, s):
            group(("d", g, s), dmat[g], slice(s * N, s * N + N))

        def quantize_d(g, s):
            nc.vector.quantize_mx(out=d_codes[s][:, g, :].bitcast(E5M2), scales=d_scales[s][:, g, :],
                                  in_=grouped["d", g, s][:].rearrange("p n j -> p (n j)"))

        def group_v(g, c):
            group(("v", g, c), vs[g], slice(c * N, c * N + N))

        def quantize_v(g, c):
            nc.vector.quantize_mx(out=v_codes[c][:, g, :].bitcast(E4M3), scales=v_scales[c][:, g, :],
                                  in_=grouped["v", g, c][:].rearrange("p n j -> p (n j)"))

        out_1v = out_1.rearrange("(g p j) m -> g j p m", g=DG, j=4)
        out_0v = out_0.rearrange("(b p) t -> b p t", p=P)
        stages = {}

        def stage_tile(key, width):
            if key not in stages:
                stages[key] = outs.tile([P, width], F32, name="stage", tag="stage")
            return stages[key]

        done = {}

        def product_1(g, j, c, engine):
            stage = stage_tile((1, g, j), M)
            bank = psum.tile([P, N], F32, name="bank_1", tag="bank")
            cols = slice(j * P, j * P + P)
            for s in range(TG):
                nc.tensor.matmul_mx(
                    out=bank[:], lhsT=dt_codes[g][:, s, cols].bitcast(E5M2), lhsT_scale=dt_scales[g][:, s, cols],
                    rhs=x_codes[c][:, s, :].bitcast(E4M3), rhs_scale=x_scales[c][:, s, :],
                    start=(s == 0), stop=(s == TG - 1))
            evac(engine, stage[:, c * N : c * N + N], bank[:])
            done[1, g, j] = done.get((1, g, j), 0) + 1
            if done[1, g, j] == MC:
                nc.sync.dma_start(out=out_1v[g, j], in_=stage[:])

        def product_0(b, s, engine):
            stage = stage_tile((0, b), T)
            c, cols, toks = b // 4, slice((b % 4) * P, (b % 4) * P + P), slice(s * N, s * N + N)
            bank = psum.tile([P, N], F32, name="bank_0", tag="bank")
            for g in range(DG):
                nc.tensor.matmul_mx(
                    out=bank[:], lhsT=v_codes[c][:, g, cols].bitcast(E4M3), lhsT_scale=v_scales[c][:, g, cols],
                    rhs=d_codes[s][:, g, :].bitcast(E5M2), rhs_scale=d_scales[s][:, g, :],
                    start=(g == 0), stop=(g == DG - 1))
            evac(engine, stage[:, toks], bank[:])
            done[0, b] = done.get((0, b), 0) + 1
            if b == 4 * MC - 1:
                nc.sync.dma_start(out=out_0v[b, :, toks], in_=stage[:, toks])
            elif done[0, b] == TG:
                nc.sync.dma_start(out=out_0v[b], in_=stage[:])

        absolute(0, 0, "S")
        mask(0, 0)
        absolute(0, 1, "S")
        mask(0, 1)
        transpose_x(0, "SVS")
        transpose_d(0, 0, "SVV")
        transpose_x(1, "VSS")
        quantize_dt(0, 0, 0)
        quantize_dt(0, 1, 0)
        quantize_dt(0, 2, 0)
        quantize_x(0, 0)
        quantize_x(0, 1)
        quantize_x(0, 2)
        absolute(0, 2, "V")
        absolute(0, 3, "S")
        mask(0, 2)
        product_1(0, 0, 0, "S")
        mask(0, 3)
        group_d(0, 0)
        transpose_x(2, "VSS")
        transpose_x(3, "SSS")
        group_d(0, 1)
        transpose_d(0, 1, "SSS")
        quantize_x(1, 0)
        quantize_x(1, 1)
        quantize_x(1, 2)
        transpose_x(4, "VSS")
        quantize_dt(0, 0, 1)
        quantize_dt(0, 1, 1)
        quantize_dt(0, 2, 1)
        transpose_x(5, "SSS")
        quantize_d(0, 0)
        absolute(1, 0, "S")
        absolute(1, 1, "S")
        product_1(0, 1, 0, "S")
        product_1(0, 2, 0, "S")
        product_1(0, 3, 0, "S")
        quantize_x(2, 0)
        quantize_x(2, 1)
        quantize_x(2, 2)
        quantize_d(0, 1)
        product_1(0, 0, 1, "S")
        mask(1, 0)
        product_1(0, 1, 1, "S")
        product_1(0, 2, 1, "S")
        product_1(0, 3, 1, "S")
        mask(1, 1)
        product_1(0, 0, 2, "S")
        transpose_d(1, 0, "SSS")
        absolute(1, 2, "V")
        mask(1, 2)
        product_1(0, 1, 2, "S")
        quantize_dt(1, 0, 0)
        quantize_dt(1, 1, 0)
        quantize_dt(1, 2, 0)
        product_1(0, 2, 2, "S")
        product_1(0, 3, 2, "S")
        absolute(1, 3, "V")
        product_1(1, 0, 0, "S")
        product_1(1, 0, 1, "S")
        product_1(1, 0, 2, "S")
        mask(1, 3)
        group_v(0, 0)
        group_d(0, 2)
        transpose_d(1, 1, "SSS")
        product_1(1, 1, 0, "S")
        product_1(1, 1, 1, "S")
        product_1(1, 1, 2, "S")
        quantize_dt(1, 0, 1)
        quantize_dt(1, 1, 1)
        quantize_dt(1, 2, 1)
        quantize_v(0, 0)
        quantize_d(0, 2)
        group_d(1, 0)
        group_v(1, 0)
        quantize_d(1, 0)
        product_1(1, 2, 0, "S")
        product_1(1, 2, 1, "S")
        product_1(1, 2, 2, "S")
        group_d(1, 1)
        quantize_v(1, 0)
        quantize_d(1, 1)
        product_1(1, 3, 0, "S")
        product_1(1, 3, 1, "S")
        product_1(1, 3, 2, "S")
        group_d(1, 2)
        quantize_d(1, 2)
        product_0(0, 0, "S")
        product_0(1, 0, "S")
        product_0(0, 1, "S")
        product_0(1, 1, "S")
        product_0(0, 2, "S")
        product_0(1, 2, "S")
        group_v(0, 1)
        group_v(1, 1)
        quantize_v(0, 1)
        product_0(2, 0, "S")
        product_0(2, 1, "S")
        product_0(2, 2, "S")
        quantize_v(1, 1)
        group_v(1, 2)
        product_0(3, 0, "S")
        product_0(3, 1, "S")
        product_0(3, 2, "S")
        group_v(0, 2)
        quantize_v(1, 2)
        product_0(4, 0, "S")
        product_0(4, 1, "S")
        product_0(4, 2, "S")
        quantize_v(0, 2)
        product_0(5, 0, "S")
        product_0(5, 1, "V")
        product_0(5, 2, "S")
        product_0(6, 0, "S")
        product_0(6, 1, "V")
        product_0(6, 2, "S")
        product_0(7, 0, "S")
        product_0(7, 1, "V")
        product_0(7, 2, "S")
        product_0(8, 0, "V")
        product_0(8, 1, "S")
        product_0(8, 2, "V")
        product_0(9, 0, "S")
        product_0(9, 1, "V")
        product_0(9, 2, "S")
        product_0(10, 0, "V")
        product_0(10, 1, "S")
        product_0(10, 2, "V")
        product_0(11, 0, "S")
        product_0(11, 1, "V")
        product_0(11, 2, "S")
